import numpy as np
import ml_dtypes


def mxq(x, axis, fmt="e4m3"):
    dtype, down = {"e4m3": (ml_dtypes.float8_e4m3fn, 7), "e5m2": (ml_dtypes.float8_e5m2, 14)}[fmt]
    v = np.moveaxis(np.asarray(x, np.float32).astype(ml_dtypes.bfloat16).astype(np.float64), axis, -1)
    blocks = v.reshape(v.shape[:-1] + (-1, 32))
    amax = np.abs(blocks).max(-1, keepdims=True)
    byte = np.maximum(np.where(amax > 0, np.frexp(amax)[1] - 1 + 127, 0) - down, 1)
    scale = np.exp2(byte - 127.0)
    codes = (blocks / scale).astype(np.float32).astype(dtype).astype(np.float64)
    return np.moveaxis((codes * scale).reshape(v.shape), -1, axis)


WIDE = False


def mx_kscale(k):
    if not WIDE:
        return np.ones(k)
    levels = np.array([10, -10, 5, -5, 0])
    if k % 512:
        return np.exp2(np.random.permutation(np.resize(levels, k // 32))).repeat(32)
    a = np.empty((k // 512, 16))
    for p in range(k // 512):
        a[p, :8] = np.random.permutation(np.resize(levels, 8))
        for g in range(8):
            far = levels[np.abs(levels - a[p, g]) >= 10]
            a[p, g + 8] = far[np.random.randint(len(far))]
    return np.exp2(a.ravel()).repeat(32)


BF16 = ml_dtypes.bfloat16


def bf(x):
    return np.asarray(x, np.float32).astype(BF16)


def f64(x):
    return np.asarray(x).astype(np.float64)


B, K, G, D, FF, F, P, H = 128, 64, 128, 2048, 4096, 2048, 7, 8
NC = K * G
EPS = 1e-5


def layernorm(x, g, b):
    m = x.mean(-1, keepdims=True)
    v = ((x - m) ** 2).mean(-1, keepdims=True)
    return (x - m) / np.sqrt(v + EPS) * g + b


def setup_inputs():
    n = np.random.standard_normal
    s, t = mx_kscale(FF), mx_kscale(D)
    return {
        "ff_hid": bf(np.maximum(n((B, K, FF)), 0.0) * s),
        "tgt": bf(n((B, K, D))),
        "w2": bf(n((FF, D)) / np.sqrt(FF) / s[:, None]),
        "b2": bf(0.1 * n(D)),
        "g3": bf((1.0 + 0.1 * n(D)) * t),
        "be3": bf(0.1 * n(D) * t),
        "dup_pool": bf(n((K, D, G)) / np.sqrt(D) / t[None, :, None]),
        "dup_bias": bf(0.2 * n(NC)),
    }


def reference(ff_hid, tgt, w2, b2, g3, be3, dup_pool, dup_bias):
    ff = (mxq(f64(ff_hid), 2, "e4m3") @ mxq(f64(w2), 0, "e4m3")) + f64(b2)
    h = layernorm(f64(tgt) + ff, f64(g3), f64(be3))
    out_extrap = (mxq(h, 2, "e4m3").transpose(1, 0, 2) @ mxq(f64(dup_pool), 1, "e4m3")).transpose(1, 0, 2)
    return out_extrap.reshape(B, -1)[:, :NC] + f64(dup_bias)

@@ -1,0 +1,352 @@
+from contextlib import ExitStack
+
+import concourse.mybir as mybir
+from concourse.masks import make_identity
+
+FLOPS = 2 * 8192 * 4096 * 2048 + 2 * 64 * 128 * 2048 * 128
+
+F32 = mybir.dt.float32
+BF16 = mybir.dt.bfloat16
+U32 = mybir.dt.uint32
+U8 = mybir.dt.uint8
+FP8X4 = mybir.dt.float8_e4m3fn_x4
+ALU = mybir.AluOpType
+ACT = mybir.ActivationFunctionType
+
+P = 128
+D = 2048
+FF = 4096
+NG = FF // 512
+NC4 = D // 512
+EPS = 1e-5
+LA = 4
+RAW4 = 4
+
+
+def tile_mldecoder_pb_l_kernel(tc, ff_hid, tgt, w2, b2, g3, be3, dup_pool, dup_bias, out):
+    nc = tc.nc
+    KT = ff_hid.shape[1]
+    with ExitStack() as ctx:
+        sb = ctx.enter_context(tc.tile_pool(name="sb", bufs=1))
+        ps = ctx.enter_context(tc.psum_pool(name="ps", bufs=1))
+        ctx.enter_context(tc.manual_schedule())
+
+        ident = sb.tile([P, P], F32, name="ident")
+        make_identity(nc, ident[:])
+        mhalf = sb.tile([P, 1], F32, name="mhalf")
+        nc.vector.memset(mhalf[:], -0.5)
+        warm = sb.tile([P, 1], F32, name="warm")
+        nc.scalar.activation(out=warm[:], in_=mhalf[:], func=ACT.Square)
+
+        w2c = [sb.tile([P, NG * 512], U32, name="w2c%d" % c, align_bytes=64) for c in range(NC4)]
+        w2s = [sb.tile([P, NG * 512], U8, name="w2s%d" % c, align_bytes=64) for c in range(NC4)]
+
+        xraw, xs, xg, xc, xsc = {}, {}, {}, {}, {}
+        traw, u, s4, nmean, ssq, rstd, vt, h = {}, {}, {}, {}, {}, {}, {}, {}
+        hg, hc, hsc, draw, dg, dc, dsc, bias, ob, wraw, wg = {}, {}, {}, {}, {}, {}, {}, {}, {}, {}, {}
+
+        def ok(i):
+            return 0 <= i < KT
+
+        def load_const(vec, nm):
+            stage = sb.tile([P, D], BF16, name="craw", tag="h", bufs=1)
+            nc.gpsimd.dma_start(out=stage[:], in_=vec.partition_broadcast(P))
+            srt = sb.tile([P, D], BF16, name=nm)
+            nc.vector.tensor_copy(
+                out=srt[:].bitcast(F32).rearrange("p (c u q) -> p c u q", c=NC4, u=2),
+                in_=stage[:].bitcast(F32).rearrange("p (c q u) -> p c u q", c=NC4, u=2),
+            )
+            return srt
+
+        def load_x(i):
+            if ok(i):
+                xraw[i] = sb.tile([P, FF], BF16, name="xraw", tag="xraw", bufs=2)
+                nc.sync.dma_start(out=xraw[i][:], in_=ff_hid[:, i, :])
+
+        def load_tgt(i):
+            if ok(i):
+                traw[i] = sb.tile([P, D], BF16, name="traw", tag="traw", bufs=2)
+                nc.sync.dma_start(out=traw[i][:], in_=tgt[:, i, :])
+
+        def load_dup(i):
+            if ok(i):
+                draw[i] = sb.tile([P, NC4, 512], BF16, name="draw", tag="raw4", bufs=RAW4)
+                nc.sync.dma_start(out=draw[i][:], in_=dup_pool[i].rearrange("(c p j) g -> p c (j g)", c=NC4, j=4))
+
+        def load_bias(q):
+            if ok(4 * q):
+                bias[q] = sb.tile([P, 512], BF16, name="bias", tag="bias", bufs=2)
+                nc.sync.dma_start(out=bias[q][:], in_=dup_bias[q * 512 : (q + 1) * 512].partition_broadcast(P))
+
+        def w2_load(m):
+            c, g = divmod(m, NG)
+            wraw[m] = sb.tile([P, 4, 512], BF16, name="wraw", tag="raw4", bufs=RAW4)
+            nc.sync.dma_start(
+                out=wraw[m][:],
+                in_=w2[g * 512 : (g + 1) * 512, c * 512 : (c + 1) * 512].rearrange("(p j) n -> p j n", j=4),
+            )
+
+        def w2_copy(m):
+            wg[m] = sb.tile([P, 2048], BF16, name="wg", tag="grp4", bufs=2, align_bytes=64)
+            src = wraw.pop(m)[:].rearrange("p j (q u e) -> p u q e j", u=2, e=2)
+            nc.vector.tensor_copy(out=wg[m][:, 0:1024].rearrange("p (q e j) -> p q e j", e=2, j=4), in_=src[:, 0])
+            nc.scalar.copy(out=wg[m][:, 1024:2048].rearrange("p (q e j) -> p q e j", e=2, j=4), in_=src[:, 1])
+
+        def w2_quant(m):
+            c, g = divmod(m, NG)
+            nc.vector.quantize_mx(
+                out=w2c[c][:, g * 512 : (g + 1) * 512].bitcast(FP8X4),
+                scales=w2s[c][:, g * 512 : (g + 1) * 512],
+                in_=wg.pop(m)[:],
+            )
+
+        def w2_step(s):
+            if s < NC4 * NG:
+                w2_copy(s)
+            if s + LA < NC4 * NG:
+                w2_load(s + LA)
+            if s >= 1:
+                w2_quant(s - 1)
+
+        def sort_x(i):
+            if ok(i):
+                xs[i] = sb.tile([P, FF // 2], F32, name="xs", tag="xs", bufs=1)
+                nc.scalar.copy(
+                    out=xs[i][:].rearrange("p (g u q) -> p g u q", g=NG, u=2),
+                    in_=xraw.pop(i)[:].bitcast(F32).rearrange("p (g q u) -> p g u q", g=NG, u=2),
+                )
+
+        def flip(block, nbanks, dst):
+            for b in range(nbanks):
+                tp = ps.tile([P, 512], F32, name="tp", tag="tp", bufs=4)
+                for s in range(4):
+                    nc.tensor.transpose(tp[:, s * P : (s + 1) * P], block(b * 4 + s), ident[:])
+                nc.scalar.copy(
+                    out=dst(b).rearrange("p (g r u) -> p g r u", g=2, u=2),
+                    in_=tp[:].rearrange("p (g u r) -> p g r u", g=2, u=2),
+                )
+
+        def flip_x(i):
+            if ok(i):
+                xg[i] = [sb.tile([P, 2048], BF16, name="xg", tag="xg", bufs=2, align_bytes=64) for hf in range(2)]
+                if i in xs:
+                    words = xs.pop(i)[:]
+                    block = lambda k: words[:, k * P : (k + 1) * P]
+                else:
+                    words = xraw.pop(i)[:].bitcast(F32)
+                    block = lambda k: words[:, (k // 2) * 256 + k % 2 : (k // 2 + 1) * 256 : 2]
+                flip(block, 4, lambda b: xg[i][b // 2][:].bitcast(F32)[:, (b % 2) * 512 : (b % 2 + 1) * 512])
+
+        def quant_x(i):
+            if ok(i):
+                xc[i] = sb.tile([P, NG * P], U32, name="xc", tag="xc", bufs=2, align_bytes=64)
+                xsc[i] = sb.tile([P, NG * P], U8, name="xsc", tag="xsc", bufs=2, align_bytes=64)
+                halves = xg.pop(i)
+                for hf in range(2):
+                    nc.vector.quantize_mx(
+                        out=xc[i][:, hf * 512 : (hf + 1) * 512].bitcast(FP8X4),
+                        scales=xsc[i][:, hf * 512 : (hf + 1) * 512],
+                        in_=halves[hf][:],
+                    )
+
+        def tgtb(i, pieces, eng):
+            if ok(i):
+                if i not in u:
+                    u[i] = sb.tile([P, D], F32, name="u", tag="u", bufs=3)
+                for c in pieces:
+                    cols = slice(c * 512, (c + 1) * 512)
+                    eng.tensor_tensor(
+                        out=u[i][:, cols].rearrange("p (u q e) -> p u q e", u=2, e=2),
+                        in0=traw[i][:, cols].rearrange("p (q u e) -> p u q e", u=2, e=2),
+                        in1=b2n[:, cols].rearrange("p (q u e) -> p u q e", u=2, e=2),
+                        op=ALU.add,
+                    )
+
+        def stage1(i, n):
+            if ok(i):
+                acc = ps.tile([P, 512], F32, name="acc", tag="acc", bufs=3)
+                for g in range(NG):
+                    nc.tensor.matmul_mx(
+                        out=acc[:],
+                        lhsT=xc[i][:, g * P : (g + 1) * P].bitcast(FP8X4),
+                        lhsT_scale=xsc[i][:, g * P : (g + 1) * P],
+                        rhs=w2c[n][:, g * 512 : (g + 1) * 512].bitcast(FP8X4),
+                        rhs_scale=w2s[n][:, g * 512 : (g + 1) * 512],
+                        start=(g == 0),
+                        stop=(g == NG - 1),
+                    )
+                return acc
+            return None
+
+        def evac(i, n, acc):
+            if ok(i):
+                if n == 0:
+                    s4[i] = sb.tile([P, NC4], F32, name="s4", tag="s4", bufs=3)
+                cols = slice(n * 512, (n + 1) * 512)
+                nc.vector.scalar_tensor_tensor(
+                    out=u[i][:, cols], in0=acc[:], scalar=1.0, in1=u[i][:, cols],
+                    op0=ALU.mult, op1=ALU.add, accum_out=s4[i][:, n : n + 1],
+                )
+
+        def ln_mean(i):
+            if ok(i):
+                nmean[i] = sb.tile([P, 1], F32, name="nmean", tag="nmean", bufs=3)
+                j4 = sb.tile([P, NC4], F32, name="j4", tag="j4", bufs=2)
+                nc.vector.tensor_scalar(
+                    out=j4[:], in0=s4.pop(i)[:], scalar1=-1.0 / D, scalar2=None,
+                    op0=ALU.mult, op1=ALU.add, accum_out=nmean[i][:],
+                )
+
+        def ln_center(i):
+            if ok(i):
+                vt[i] = sb.tile([P, D], F32, name="vt", tag="vt", bufs=1)
+                nc.vector.scalar_tensor_tensor(
+                    out=vt[i][:], in0=u[i][:], scalar=nmean[i][:], in1=late["g3s"][:], op0=ALU.add, op1=ALU.mult,
+                )
+
+        def ln_square(i):
+            if ok(i):
+                ssq[i] = sb.tile([P, 1], F32, name="ssq", tag="ssq", bufs=3)
+                junk = sb.tile([P, D], BF16, name="junk", tag="h", bufs=1)
+                nc.scalar.activation(
+                    out=junk[:], in_=u.pop(i)[:], func=ACT.Square, bias=nmean.pop(i)[:], scale=1.0, accum_out=ssq[i][:],
+                )
+
+        def ln_rstd(i):
+            if ok(i):
+                tv = sb.tile([P, 1], F32, name="tv", tag="tv", bufs=2)
+                rstd[i] = sb.tile([P, 1], F32, name="rstd", tag="rstd", bufs=3)
+                nc.gpsimd.tensor_scalar(out=tv[:], in0=ssq.pop(i)[:], scalar1=1.0 / D, scalar2=EPS, op0=ALU.mult, op1=ALU.add)
+                nc.gpsimd.tensor_tensor(out=rstd[i][:], in0=tv[:], in1=mhalf[:], op=ALU.pow)
+
+        def ln_out(i):
+            if ok(i):
+                h[i] = sb.tile([P, D], BF16, name="h", tag="h", bufs=1)
+                nc.vector.scalar_tensor_tensor(
+                    out=h[i][:], in0=vt.pop(i)[:], scalar=rstd.pop(i)[:], in1=late["be3s"][:], op0=ALU.mult, op1=ALU.add,
+                )
+
+        def flip_h(i):
+            if ok(i):
+                hg[i] = sb.tile([P, 2048], BF16, name="hg", tag="hg", bufs=1, align_bytes=64)
+                words = h.pop(i)[:].bitcast(F32)
+                flip(lambda k: words[:, k * P : (k + 1) * P], 2, lambda b: hg[i][:].bitcast(F32)[:, b * 512 : (b + 1) * 512])
+
+        def quant_h(i):
+            if ok(i):
+                hc[i] = sb.tile([P, 512], U32, name="hc", tag="hc", bufs=2, align_bytes=64)
+                hsc[i] = sb.tile([P, 512], U8, name="hsc", tag="hsc", bufs=2, align_bytes=64)
+                nc.vector.quantize_mx(out=hc[i][:].bitcast(FP8X4), scales=hsc[i][:], in_=hg.pop(i)[:])
+
+        def inter_dup(i):
+            if ok(i):
+                dg[i] = sb.tile([P, 2048], BF16, name="dg", tag="grp4", bufs=2, align_bytes=64)
+                nc.scalar.copy(
+                    out=dg[i][:].rearrange("p (c g j) -> p c g j", c=NC4, j=4),
+                    in_=draw.pop(i)[:].rearrange("p c (j g) -> p c g j", j=4),
+                )
+
+        def quant_dup(i):
+            if ok(i):
+                dc[i] = sb.tile([P, 512], U32, name="dc", tag="dc", bufs=2, align_bytes=64)
+                dsc[i] = sb.tile([P, 512], U8, name="dsc", tag="dsc", bufs=2, align_bytes=64)
+                nc.vector.quantize_mx(out=dc[i][:].bitcast(FP8X4), scales=dsc[i][:], in_=dg.pop(i)[:])
+
+        def stage2(i):
+            if ok(i):
+                q, r = divmod(i, 4)
+                if r == 0:
+                    ob[q] = ps.tile([P, 512], F32, name="ob", tag="ob", bufs=1)
+                for c in range(NC4):
+                    nc.tensor.matmul_mx(
+                        out=ob[q][:, r * P : (r + 1) * P],
+                        lhsT=hc[i][:, c * P : (c + 1) * P].bitcast(FP8X4),
+                        lhsT_scale=hsc[i][:, c * P : (c + 1) * P],
+                        rhs=dc[i][:, c * P : (c + 1) * P].bitcast(FP8X4),
+                        rhs_scale=dsc[i][:, c * P : (c + 1) * P],
+                        start=(c == 0),
+                        stop=(c == NC4 - 1),
+                    )
+
+        def store(i):
+            if ok(i) and i % 4 == 3:
+                q = i // 4
+                ot = sb.tile([P, 512], F32, name="ot", tag="ot", bufs=2)
+                nc.vector.tensor_tensor(out=ot[:], in0=ob.pop(q)[:], in1=bias.pop(q)[:], op=ALU.add)
+                ready[q] = ot
+
+        def store_dma(i):
+            if ok(i) and i % 4 == 3:
+                q = i // 4
+                nc.sync.dma_start(out=out[:, q * 512 : (q + 1) * 512], in_=ready.pop(q)[:])
+
+        late = {}
+        ready = {}
+        load_x(0)
+        for m in range(LA):
+            w2_load(m)
+        b2n = sb.tile([P, D], BF16, name="b2n")
+        nc.sync.dma_start(out=b2n[:], in_=b2.partition_broadcast(P))
+        load_tgt(0)
+        flip_x(0)
+
+        for i in range(0, KT + 4):
+            if i > 0:
+                load_x(i + 3)
+                load_tgt(i + 2)
+                if i % 4 == 0:
+                    load_bias(i // 4)
+                store_dma(i - 3)
+                flip_x(i + 1)
+            flip_h(i - 2)
+
+            ln_mean(i - 1)
+            ln_center(i - 1)
+            ln_square(i - 1)
+            if i > 0:
+                tgtb(i + 1, (0, 1), nc.gpsimd)
+            ln_rstd(i - 1)
+            if i > 0:
+                tgtb(i + 1, (2, 3), nc.gpsimd)
+
+            for n in range(NC4):
+                if i == 0:
+                    for s in range(0 if n == 0 else NG * n + 1, NG * n + NG + 1):
+                        w2_step(s)
+                        if s == 1:
+                            quant_x(0)
+                        if s == 5:
+                            tgtb(0, (0, 1, 2, 3), nc.vector)
+                        if s == 12:
+                            load_x(1)
+                            load_tgt(1)
+                acc = stage1(i, n)
+                if n == 0 and i > 0:
+                    quant_x(i + 1)
+                if n == 1:
+                    quant_h(i - 2)
+                if n == 2:
+                    if i == 0:
+                        flip_x(1)
+                        tgtb(1, (0, 1, 2, 3), nc.vector)
+                        load_x(2)
+                        load_bias(0)
+                    if i > 0:
+                        sort_x(i + 2)
+                    inter_dup(i - 1)
+                evac(i, n, acc)
+                if n == 1:
+                    stage2(i - 2)
+                    ln_out(i - 1)
+                if n == 2:
+                    store(i - 2)
+                    quant_dup(i - 1)
+                    if i == 0:
+                        quant_x(1)
+            load_dup(i)
+            if i == 0:
+                sort_x(2)
+                load_x(3)
+                load_tgt(2)
+                late["g3s"] = load_const(g3, "g3s")
+                late["be3s"] = load_const(be3, "be3s")

@@ -48,9 +48,12 @@ def tile_mldecoder_pb_l_kernel(tc, ff_hid, tgt, w2, b2, g3, be3, dup_pool, dup_b
         def ok(i):
             return 0 <= i < KT
 
-        def load_const(vec, nm):
-            stage = sb.tile([P, D], BF16, name="craw", tag="h", bufs=1)
+        def load_const(vec, tag, align):
+            stage = sb.tile([P, D], BF16, name="craw", tag=tag, bufs=1, align_bytes=align)
             nc.gpsimd.dma_start(out=stage[:], in_=vec.partition_broadcast(P))
+            return stage
+
+        def sort_const(stage, nm):
             srt = sb.tile([P, D], BF16, name=nm)
             nc.vector.tensor_copy(
                 out=srt[:].bitcast(F32).rearrange("p (c u q) -> p c u q", c=NC4, u=2),
@@ -288,6 +291,8 @@ def tile_mldecoder_pb_l_kernel(tc, ff_hid, tgt, w2, b2, g3, be3, dup_pool, dup_b
         b2n = sb.tile([P, D], BF16, name="b2n")
         nc.sync.dma_start(out=b2n[:], in_=b2.partition_broadcast(P))
         load_tgt(0)
+        g3raw = load_const(g3, "h", None)
+        be3raw = load_const(be3, "hg", 64)
         flip_x(0)
 
         for i in range(0, KT + 4):
@@ -303,11 +308,7 @@ def tile_mldecoder_pb_l_kernel(tc, ff_hid, tgt, w2, b2, g3, be3, dup_pool, dup_b
             ln_mean(i - 1)
             ln_center(i - 1)
             ln_square(i - 1)
-            if i > 0:
-                tgtb(i + 1, (0, 1), nc.gpsimd)
             ln_rstd(i - 1)
-            if i > 0:
-                tgtb(i + 1, (2, 3), nc.gpsimd)
 
             for n in range(NC4):
                 if i == 0:
@@ -317,12 +318,17 @@ def tile_mldecoder_pb_l_kernel(tc, ff_hid, tgt, w2, b2, g3, be3, dup_pool, dup_b
                             quant_x(0)
                         if s == 5:
                             tgtb(0, (0, 1, 2, 3), nc.vector)
+                        if s == 20:
+                            late["g3s"] = sort_const(g3raw, "g3s")
+                        if s == 28:
+                            late["be3s"] = sort_const(be3raw, "be3s")
                         if s == 12:
                             load_x(1)
                             load_tgt(1)
                 acc = stage1(i, n)
                 if n == 0 and i > 0:
                     quant_x(i + 1)
+                    tgtb(i + 1, (0, 1), nc.vector)
                 if n == 1:
                     quant_h(i - 2)
                 if n == 2:
@@ -337,6 +343,8 @@ def tile_mldecoder_pb_l_kernel(tc, ff_hid, tgt, w2, b2, g3, be3, dup_pool, dup_b
                 evac(i, n, acc)
                 if n == 1:
                     stage2(i - 2)
+                    if i > 0:
+                        tgtb(i + 1, (2, 3), nc.vector)
                     ln_out(i - 1)
                 if n == 2:
                     store(i - 2)
@@ -348,5 +356,3 @@ def tile_mldecoder_pb_l_kernel(tc, ff_hid, tgt, w2, b2, g3, be3, dup_pool, dup_b
                 sort_x(2)
                 load_x(3)
                 load_tgt(2)
-                late["g3s"] = load_const(g3, "g3s")
-                late["be3s"] = load_const(be3, "be3s")

@@ -121,7 +121,7 @@ def tile_mldecoder_pb_l_kernel(tc, ff_hid, tgt, w2, b2, g3, be3, dup_pool, dup_b
 
         def flip(block, nbanks, dst):
             for b in range(nbanks):
-                tp = ps.tile([P, 512], F32, name="tp", tag="tp", bufs=4)
+                tp = ps.tile([P, 512], F32, name="tp", tag="tp", bufs=5)
                 for s in range(4):
                     nc.tensor.transpose(tp[:, s * P : (s + 1) * P], block(b * 4 + s), ident[:])
                 nc.scalar.copy(
@@ -257,12 +257,10 @@ def tile_mldecoder_pb_l_kernel(tc, ff_hid, tgt, w2, b2, g3, be3, dup_pool, dup_b
 
         def stage2(i):
             if ok(i):
-                q, r = divmod(i, 4)
-                if r == 0:
-                    ob[q] = ps.tile([P, 512], F32, name="ob", tag="ob", bufs=1)
+                ob[i] = ps.tile([P, 512], F32, name="ob", tag="acc", bufs=3)
                 for c in range(NC4):
                     nc.tensor.matmul_mx(
-                        out=ob[q][:, r * P : (r + 1) * P],
+                        out=ob[i][:, 0:P],
                         lhsT=hc[i][:, c * P : (c + 1) * P].bitcast(FP8X4),
                         lhsT_scale=hsc[i][:, c * P : (c + 1) * P],
                         rhs=dc[i][:, c * P : (c + 1) * P].bitcast(FP8X4),
@@ -272,15 +270,17 @@ def tile_mldecoder_pb_l_kernel(tc, ff_hid, tgt, w2, b2, g3, be3, dup_pool, dup_b
                     )
 
         def store(i):
-            if ok(i) and i % 4 == 3:
-                q = i // 4
-                ot = sb.tile([P, 512], F32, name="ot", tag="ot", bufs=2)
-                nc.vector.tensor_tensor(out=ot[:], in0=ob.pop(q)[:], in1=bias.pop(q)[:], op=ALU.add)
-                ready[q] = ot
+            if ok(i):
+                q, r = divmod(i, 4)
+                if r == 0:
+                    ready[q] = sb.tile([P, 512], F32, name="ot", tag="ot", bufs=2)
+                cols = slice(r * P, (r + 1) * P)
+                nc.vector.tensor_tensor(out=ready[q][:, cols], in0=ob.pop(i)[:, 0:P], in1=bias[q][:, cols], op=ALU.add)
 
         def store_dma(i):
             if ok(i) and i % 4 == 3:
                 q = i // 4
+                bias.pop(q)
                 nc.sync.dma_start(out=out[:, q * 512 : (q + 1) * 512], in_=ready.pop(q)[:])
 
         late = {}
@@ -305,7 +305,11 @@ def tile_mldecoder_pb_l_kernel(tc, ff_hid, tgt, w2, b2, g3, be3, dup_pool, dup_b
                 flip_x(i + 1)
             flip_h(i - 2)
 
+            if i > 0:
+                tgtb(i + 1, (0,), nc.vector)
             ln_mean(i - 1)
+            if i > 0:
+                tgtb(i + 1, (1,), nc.vector)
             ln_center(i - 1)
             ln_square(i - 1)
             ln_rstd(i - 1)
@@ -328,9 +332,10 @@ def tile_mldecoder_pb_l_kernel(tc, ff_hid, tgt, w2, b2, g3, be3, dup_pool, dup_b
                 acc = stage1(i, n)
                 if n == 0 and i > 0:
                     quant_x(i + 1)
-                    tgtb(i + 1, (0, 1), nc.vector)
                 if n == 1:
                     quant_h(i - 2)
+                    if i > 0:
+                        tgtb(i + 1, (2,), nc.vector)
                 if n == 2:
                     if i == 0:
                         flip_x(1)
@@ -344,7 +349,7 @@ def tile_mldecoder_pb_l_kernel(tc, ff_hid, tgt, w2, b2, g3, be3, dup_pool, dup_b
                 if n == 1:
                     stage2(i - 2)
                     if i > 0:
-                        tgtb(i + 1, (2, 3), nc.vector)
+                        tgtb(i + 1, (3,), nc.vector)
                     ln_out(i - 1)
                 if n == 2:
                     store(i - 2)

@@ -50,7 +50,7 @@ def tile_mldecoder_pb_l_kernel(tc, ff_hid, tgt, w2, b2, g3, be3, dup_pool, dup_b
 
         def load_const(vec, tag, align):
             stage = sb.tile([P, D], BF16, name="craw", tag=tag, bufs=1, align_bytes=align)
-            nc.gpsimd.dma_start(out=stage[:], in_=vec.partition_broadcast(P))
+            nc.sync.dma_start(out=stage[:], in_=vec.partition_broadcast(P))
             return stage
 
         def sort_const(stage, nm):
@@ -90,7 +90,7 @@ def tile_mldecoder_pb_l_kernel(tc, ff_hid, tgt, w2, b2, g3, be3, dup_pool, dup_b
             )
 
         def w2_copy(m):
-            wg[m] = sb.tile([P, 2048], BF16, name="wg", tag="grp4", bufs=2, align_bytes=64)
+            wg[m] = sb.tile([P, 2048], BF16, name="wg", tag="grp4", bufs=3, align_bytes=64)
             src = wraw.pop(m)[:].rearrange("p j (q u e) -> p u q e j", u=2, e=2)
             nc.vector.tensor_copy(out=wg[m][:, 0:1024].rearrange("p (q e j) -> p q e j", e=2, j=4), in_=src[:, 0])
             nc.scalar.copy(out=wg[m][:, 1024:2048].rearrange("p (q e j) -> p q e j", e=2, j=4), in_=src[:, 1])
@@ -131,26 +131,20 @@ def tile_mldecoder_pb_l_kernel(tc, ff_hid, tgt, w2, b2, g3, be3, dup_pool, dup_b
 
         def flip_x(i):
             if ok(i):
-                xg[i] = [sb.tile([P, 2048], BF16, name="xg", tag="xg", bufs=2, align_bytes=64) for hf in range(2)]
+                xg[i] = sb.tile([P, FF], BF16, name="xg", tag="xg", bufs=1, align_bytes=64)
                 if i in xs:
                     words = xs.pop(i)[:]
                     block = lambda k: words[:, k * P : (k + 1) * P]
                 else:
                     words = xraw.pop(i)[:].bitcast(F32)
                     block = lambda k: words[:, (k // 2) * 256 + k % 2 : (k // 2 + 1) * 256 : 2]
-                flip(block, 4, lambda b: xg[i][b // 2][:].bitcast(F32)[:, (b % 2) * 512 : (b % 2 + 1) * 512])
+                flip(block, 4, lambda b: xg[i][:].bitcast(F32)[:, b * 512 : (b + 1) * 512])
 
         def quant_x(i):
             if ok(i):
                 xc[i] = sb.tile([P, NG * P], U32, name="xc", tag="xc", bufs=2, align_bytes=64)
                 xsc[i] = sb.tile([P, NG * P], U8, name="xsc", tag="xsc", bufs=2, align_bytes=64)
-                halves = xg.pop(i)
-                for hf in range(2):
-                    nc.vector.quantize_mx(
-                        out=xc[i][:, hf * 512 : (hf + 1) * 512].bitcast(FP8X4),
-                        scales=xsc[i][:, hf * 512 : (hf + 1) * 512],
-                        in_=halves[hf][:],
-                    )
+                nc.vector.quantize_mx(out=xc[i][:].bitcast(FP8X4), scales=xsc[i][:], in_=xg.pop(i)[:])
 
         def tgtb(i, pieces, eng):
             if ok(i):
@@ -243,7 +237,7 @@ def tile_mldecoder_pb_l_kernel(tc, ff_hid, tgt, w2, b2, g3, be3, dup_pool, dup_b
 
         def inter_dup(i):
             if ok(i):
-                dg[i] = sb.tile([P, 2048], BF16, name="dg", tag="grp4", bufs=2, align_bytes=64)
+                dg[i] = sb.tile([P, 2048], BF16, name="dg", tag="grp4", bufs=3, align_bytes=64)
                 nc.scalar.copy(
                     out=dg[i][:].rearrange("p (c g j) -> p c g j", c=NC4, j=4),
                     in_=draw.pop(i)[:].rearrange("p c (j g) -> p c g j", j=4),
@@ -291,8 +285,6 @@ def tile_mldecoder_pb_l_kernel(tc, ff_hid, tgt, w2, b2, g3, be3, dup_pool, dup_b
         b2n = sb.tile([P, D], BF16, name="b2n")
         nc.sync.dma_start(out=b2n[:], in_=b2.partition_broadcast(P))
         load_tgt(0)
-        g3raw = load_const(g3, "h", None)
-        be3raw = load_const(be3, "hg", 64)
         flip_x(0)
 
         for i in range(0, KT + 4):
@@ -322,10 +314,13 @@ def tile_mldecoder_pb_l_kernel(tc, ff_hid, tgt, w2, b2, g3, be3, dup_pool, dup_b
                             quant_x(0)
                         if s == 5:
                             tgtb(0, (0, 1, 2, 3), nc.vector)
-                        if s == 20:
-                            late["g3s"] = sort_const(g3raw, "g3s")
-                        if s == 28:
-                            late["be3s"] = sort_const(be3raw, "be3s")
+                        if s == 14:
+                            late["g3raw"] = load_const(g3, "h", None)
+                            late["be3raw"] = load_const(be3, "hg", 64)
+                        if s == 24:
+                            late["g3s"] = sort_const(late["g3raw"], "g3s")
+                        if s == 30:
+                            late["be3s"] = sort_const(late["be3raw"], "be3s")
                         if s == 12:
                             load_x(1)
                             load_tgt(1)

@@ -342,13 +342,14 @@ def tile_mldecoder_pb_l_kernel(tc, ff_hid, tgt, w2, b2, g3, be3, dup_pool, dup_b
                     inter_dup(i - 1)
                 evac(i, n, acc)
                 if n == 1:
-                    stage2(i - 2)
                     if i > 0:
                         tgtb(i + 1, (3,), nc.vector)
                     ln_out(i - 1)
                 if n == 2:
-                    store(i - 2)
+                    stage2(i - 2)
                     quant_dup(i - 1)
+                if n == 3:
+                    store(i - 2)
                     if i == 0:
                         quant_x(1)
             load_dup(i)

from contextlib import ExitStack

import concourse.mybir as mybir
from concourse.masks import make_identity

FLOPS = 2 * 8192 * 4096 * 2048 + 2 * 64 * 128 * 2048 * 128

F32 = mybir.dt.float32
BF16 = mybir.dt.bfloat16
U32 = mybir.dt.uint32
U8 = mybir.dt.uint8
FP8X4 = mybir.dt.float8_e4m3fn_x4
ALU = mybir.AluOpType
ACT = mybir.ActivationFunctionType

P = 128
D = 2048
FF = 4096
NG = FF // 512
NC4 = D // 512
EPS = 1e-5
LA = 4
RAW4 = 4


def tile_mldecoder_pb_l_kernel(tc, ff_hid, tgt, w2, b2, g3, be3, dup_pool, dup_bias, out):
    nc = tc.nc
    KT = ff_hid.shape[1]
    with ExitStack() as ctx:
        sb = ctx.enter_context(tc.tile_pool(name="sb", bufs=1))
        ps = ctx.enter_context(tc.psum_pool(name="ps", bufs=1))
        ctx.enter_context(tc.manual_schedule())

        ident = sb.tile([P, P], F32, name="ident")
        make_identity(nc, ident[:])
        mhalf = sb.tile([P, 1], F32, name="mhalf")
        nc.vector.memset(mhalf[:], -0.5)
        warm = sb.tile([P, 1], F32, name="warm")
        nc.scalar.activation(out=warm[:], in_=mhalf[:], func=ACT.Square)

        w2c = [sb.tile([P, NG * 512], U32, name="w2c%d" % c, align_bytes=64) for c in range(NC4)]
        w2s = [sb.tile([P, NG * 512], U8, name="w2s%d" % c, align_bytes=64) for c in range(NC4)]

        xraw, xs, xg, xc, xsc = {}, {}, {}, {}, {}
        traw, u, s4, nmean, ssq, rstd, vt, h = {}, {}, {}, {}, {}, {}, {}, {}
        hg, hc, hsc, draw, dg, dc, dsc, bias, ob, wraw, wg = {}, {}, {}, {}, {}, {}, {}, {}, {}, {}, {}

        def ok(i):
            return 0 <= i < KT

        def load_const(vec, tag, align):
            stage = sb.tile([P, D], BF16, name="craw", tag=tag, bufs=1, align_bytes=align)
            nc.sync.dma_start(out=stage[:], in_=vec.partition_broadcast(P))
            return stage

        def sort_const(stage, nm):
            srt = sb.tile([P, D], BF16, name=nm)
            nc.vector.tensor_copy(
                out=srt[:].bitcast(F32).rearrange("p (c u q) -> p c u q", c=NC4, u=2),
                in_=stage[:].bitcast(F32).rearrange("p (c q u) -> p c u q", c=NC4, u=2),
            )
            return srt

        def load_x(i):
            if ok(i):
                xraw[i] = sb.tile([P, FF], BF16, name="xraw", tag="xraw", bufs=2)
                nc.sync.dma_start(out=xraw[i][:], in_=ff_hid[:, i, :])

        def load_tgt(i):
            if ok(i):
                traw[i] = sb.tile([P, D], BF16, name="traw", tag="traw", bufs=2)
                nc.sync.dma_start(out=traw[i][:], in_=tgt[:, i, :])

        def load_dup(i):
            if ok(i):
                draw[i] = sb.tile([P, NC4, 512], BF16, name="draw", tag="raw4", bufs=RAW4)
                nc.sync.dma_start(out=draw[i][:], in_=dup_pool[i].rearrange("(c p j) g -> p c (j g)", c=NC4, j=4))

        def load_bias(q):
            if ok(4 * q):
                bias[q] = sb.tile([P, 512], BF16, name="bias", tag="bias", bufs=2)
                nc.sync.dma_start(out=bias[q][:], in_=dup_bias[q * 512 : (q + 1) * 512].partition_broadcast(P))

        def w2_load(m):
            c, g = divmod(m, NG)
            wraw[m] = sb.tile([P, 4, 512], BF16, name="wraw", tag="raw4", bufs=RAW4)
            nc.sync.dma_start(
                out=wraw[m][:],
                in_=w2[g * 512 : (g + 1) * 512, c * 512 : (c + 1) * 512].rearrange("(p j) n -> p j n", j=4),
            )

        def w2_copy(m):
            wg[m] = sb.tile([P, 2048], BF16, name="wg", tag="grp4", bufs=3, align_bytes=64)
            src = wraw.pop(m)[:].rearrange("p j (q u e) -> p u q e j", u=2, e=2)
            nc.vector.tensor_copy(out=wg[m][:, 0:1024].rearrange("p (q e j) -> p q e j", e=2, j=4), in_=src[:, 0])
            nc.scalar.copy(out=wg[m][:, 1024:2048].rearrange("p (q e j) -> p q e j", e=2, j=4), in_=src[:, 1])

        def w2_quant(m):
            c, g = divmod(m, NG)
            nc.vector.quantize_mx(
                out=w2c[c][:, g * 512 : (g + 1) * 512].bitcast(FP8X4),
                scales=w2s[c][:, g * 512 : (g + 1) * 512],
                in_=wg.pop(m)[:],
            )

        def w2_step(s):
            if s < NC4 * NG:
                w2_copy(s)
            if s + LA < NC4 * NG:
                w2_load(s + LA)
            if s >= 1:
                w2_quant(s - 1)

        def sort_x(i):
            if ok(i):
                xs[i] = sb.tile([P, FF // 2], F32, name="xs", tag="xs", bufs=1)
                nc.scalar.copy(
                    out=xs[i][:].rearrange("p (g u q) -> p g u q", g=NG, u=2),
                    in_=xraw.pop(i)[:].bitcast(F32).rearrange("p (g q u) -> p g u q", g=NG, u=2),
                )

        def flip(block, nbanks, dst):
            for b in range(nbanks):
                tp = ps.tile([P, 512], F32, name="tp", tag="tp", bufs=5)
                for s in range(4):
                    nc.tensor.transpose(tp[:, s * P : (s + 1) * P], block(b * 4 + s), ident[:])
                nc.scalar.copy(
                    out=dst(b).rearrange("p (g r u) -> p g r u", g=2, u=2),
                    in_=tp[:].rearrange("p (g u r) -> p g r u", g=2, u=2),
                )

        def flip_x(i):
            if ok(i):
                xg[i] = sb.tile([P, FF], BF16, name="xg", tag="xg", bufs=1, align_bytes=64)
                if i in xs:
                    words = xs.pop(i)[:]
                    block = lambda k: words[:, k * P : (k + 1) * P]
                else:
                    words = xraw.pop(i)[:].bitcast(F32)
                    block = lambda k: words[:, (k // 2) * 256 + k % 2 : (k // 2 + 1) * 256 : 2]
                flip(block, 4, lambda b: xg[i][:].bitcast(F32)[:, b * 512 : (b + 1) * 512])

        def quant_x(i):
            if ok(i):
                xc[i] = sb.tile([P, NG * P], U32, name="xc", tag="xc", bufs=2, align_bytes=64)
                xsc[i] = sb.tile([P, NG * P], U8, name="xsc", tag="xsc", bufs=2, align_bytes=64)
                nc.vector.quantize_mx(out=xc[i][:].bitcast(FP8X4), scales=xsc[i][:], in_=xg.pop(i)[:])

        def tgtb(i, pieces, eng):
            if ok(i):
                if i not in u:
                    u[i] = sb.tile([P, D], F32, name="u", tag="u", bufs=3)
                for c in pieces:
                    cols = slice(c * 512, (c + 1) * 512)
                    eng.tensor_tensor(
                        out=u[i][:, cols].rearrange("p (u q e) -> p u q e", u=2, e=2),
                        in0=traw[i][:, cols].rearrange("p (q u e) -> p u q e", u=2, e=2),
                        in1=b2n[:, cols].rearrange("p (q u e) -> p u q e", u=2, e=2),
                        op=ALU.add,
                    )

        def stage1(i, n):
            if ok(i):
                acc = ps.tile([P, 512], F32, name="acc", tag="acc", bufs=3)
                for g in range(NG):
                    nc.tensor.matmul_mx(
                        out=acc[:],
                        lhsT=xc[i][:, g * P : (g + 1) * P].bitcast(FP8X4),
                        lhsT_scale=xsc[i][:, g * P : (g + 1) * P],
                        rhs=w2c[n][:, g * 512 : (g + 1) * 512].bitcast(FP8X4),
                        rhs_scale=w2s[n][:, g * 512 : (g + 1) * 512],
                        start=(g == 0),
                        stop=(g == NG - 1),
                    )
                return acc
            return None

        def evac(i, n, acc):
            if ok(i):
                if n == 0:
                    s4[i] = sb.tile([P, NC4], F32, name="s4", tag="s4", bufs=3)
                cols = slice(n * 512, (n + 1) * 512)
                nc.vector.scalar_tensor_tensor(
                    out=u[i][:, cols], in0=acc[:], scalar=1.0, in1=u[i][:, cols],
                    op0=ALU.mult, op1=ALU.add, accum_out=s4[i][:, n : n + 1],
                )

        def ln_mean(i):
            if ok(i):
                nmean[i] = sb.tile([P, 1], F32, name="nmean", tag="nmean", bufs=3)
                j4 = sb.tile([P, NC4], F32, name="j4", tag="j4", bufs=2)
                nc.vector.tensor_scalar(
                    out=j4[:], in0=s4.pop(i)[:], scalar1=-1.0 / D, scalar2=None,
                    op0=ALU.mult, op1=ALU.add, accum_out=nmean[i][:],
                )

        def ln_center(i):
            if ok(i):
                vt[i] = sb.tile([P, D], F32, name="vt", tag="vt", bufs=1)
                nc.vector.scalar_tensor_tensor(
                    out=vt[i][:], in0=u[i][:], scalar=nmean[i][:], in1=late["g3s"][:], op0=ALU.add, op1=ALU.mult,
                )

        def ln_square(i):
            if ok(i):
                ssq[i] = sb.tile([P, 1], F32, name="ssq", tag="ssq", bufs=3)
                junk = sb.tile([P, D], BF16, name="junk", tag="h", bufs=1)
                nc.scalar.activation(
                    out=junk[:], in_=u.pop(i)[:], func=ACT.Square, bias=nmean.pop(i)[:], scale=1.0, accum_out=ssq[i][:],
                )

        def ln_rstd(i):
            if ok(i):
                tv = sb.tile([P, 1], F32, name="tv", tag="tv", bufs=2)
                rstd[i] = sb.tile([P, 1], F32, name="rstd", tag="rstd", bufs=3)
                nc.gpsimd.tensor_scalar(out=tv[:], in0=ssq.pop(i)[:], scalar1=1.0 / D, scalar2=EPS, op0=ALU.mult, op1=ALU.add)
                nc.gpsimd.tensor_tensor(out=rstd[i][:], in0=tv[:], in1=mhalf[:], op=ALU.pow)

        def ln_out(i):
            if ok(i):
                h[i] = sb.tile([P, D], BF16, name="h", tag="h", bufs=1)
                nc.vector.scalar_tensor_tensor(
                    out=h[i][:], in0=vt.pop(i)[:], scalar=rstd.pop(i)[:], in1=late["be3s"][:], op0=ALU.mult, op1=ALU.add,
                )

        def flip_h(i):
            if ok(i):
                hg[i] = sb.tile([P, 2048], BF16, name="hg", tag="hg", bufs=1, align_bytes=64)
                words = h.pop(i)[:].bitcast(F32)
                flip(lambda k: words[:, k * P : (k + 1) * P], 2, lambda b: hg[i][:].bitcast(F32)[:, b * 512 : (b + 1) * 512])

        def quant_h(i):
            if ok(i):
                hc[i] = sb.tile([P, 512], U32, name="hc", tag="hc", bufs=2, align_bytes=64)
                hsc[i] = sb.tile([P, 512], U8, name="hsc", tag="hsc", bufs=2, align_bytes=64)
                nc.vector.quantize_mx(out=hc[i][:].bitcast(FP8X4), scales=hsc[i][:], in_=hg.pop(i)[:])

        def inter_dup(i):
            if ok(i):
                dg[i] = sb.tile([P, 2048], BF16, name="dg", tag="grp4", bufs=3, align_bytes=64)
                nc.scalar.copy(
                    out=dg[i][:].rearrange("p (c g j) -> p c g j", c=NC4, j=4),
                    in_=draw.pop(i)[:].rearrange("p c (j g) -> p c g j", j=4),
                )

        def quant_dup(i):
            if ok(i):
                dc[i] = sb.tile([P, 512], U32, name="dc", tag="dc", bufs=2, align_bytes=64)
                dsc[i] = sb.tile([P, 512], U8, name="dsc", tag="dsc", bufs=2, align_bytes=64)
                nc.vector.quantize_mx(out=dc[i][:].bitcast(FP8X4), scales=dsc[i][:], in_=dg.pop(i)[:])

        def stage2(i):
            if ok(i):
                ob[i] = ps.tile([P, 512], F32, name="ob", tag="acc", bufs=3)
                for c in range(NC4):
                    nc.tensor.matmul_mx(
                        out=ob[i][:, 0:P],
                        lhsT=hc[i][:, c * P : (c + 1) * P].bitcast(FP8X4),
                        lhsT_scale=hsc[i][:, c * P : (c + 1) * P],
                        rhs=dc[i][:, c * P : (c + 1) * P].bitcast(FP8X4),
                        rhs_scale=dsc[i][:, c * P : (c + 1) * P],
                        start=(c == 0),
                        stop=(c == NC4 - 1),
                    )

        def store(i):
            if ok(i):
                q, r = divmod(i, 4)
                if r == 0:
                    ready[q] = sb.tile([P, 512], F32, name="ot", tag="ot", bufs=2)
                cols = slice(r * P, (r + 1) * P)
                nc.vector.tensor_tensor(out=ready[q][:, cols], in0=ob.pop(i)[:, 0:P], in1=bias[q][:, cols], op=ALU.add)

        def store_dma(i):
            if ok(i) and i % 4 == 3:
                q = i // 4
                bias.pop(q)
                nc.sync.dma_start(out=out[:, q * 512 : (q + 1) * 512], in_=ready.pop(q)[:])

        late = {}
        ready = {}
        load_x(0)
        for m in range(LA):
            w2_load(m)
        b2n = sb.tile([P, D], BF16, name="b2n")
        nc.sync.dma_start(out=b2n[:], in_=b2.partition_broadcast(P))
        load_tgt(0)
        flip_x(0)

        for i in range(0, KT + 4):
            if i > 0:
                load_x(i + 3)
                load_tgt(i + 2)
                if i % 4 == 0:
                    load_bias(i // 4)
                store_dma(i - 3)
                flip_x(i + 1)
            flip_h(i - 2)

            if i > 0:
                tgtb(i + 1, (0,), nc.vector)
            ln_mean(i - 1)
            if i > 0:
                tgtb(i + 1, (1,), nc.vector)
            ln_center(i - 1)
            ln_square(i - 1)
            ln_rstd(i - 1)

            for n in range(NC4):
                if i == 0:
                    for s in range(0 if n == 0 else NG * n + 1, NG * n + NG + 1):
                        w2_step(s)
                        if s == 1:
                            quant_x(0)
                        if s == 5:
                            tgtb(0, (0, 1, 2, 3), nc.vector)
                        if s == 14:
                            late["g3raw"] = load_const(g3, "h", None)
                            late["be3raw"] = load_const(be3, "hg", 64)
                        if s == 24:
                            late["g3s"] = sort_const(late["g3raw"], "g3s")
                        if s == 30:
                            late["be3s"] = sort_const(late["be3raw"], "be3s")
                        if s == 12:
                            load_x(1)
                            load_tgt(1)
                acc = stage1(i, n)
                if n == 0 and i > 0:
                    quant_x(i + 1)
                if n == 1:
                    quant_h(i - 2)
                    if i > 0:
                        tgtb(i + 1, (2,), nc.vector)
                if n == 2:
                    if i == 0:
                        flip_x(1)
                        tgtb(1, (0, 1, 2, 3), nc.vector)
                        load_x(2)
                        load_bias(0)
                    if i > 0:
                        sort_x(i + 2)
                    inter_dup(i - 1)
                evac(i, n, acc)
                if n == 1:
                    if i > 0:
                        tgtb(i + 1, (3,), nc.vector)
                    ln_out(i - 1)
                if n == 2:
                    stage2(i - 2)
                    quant_dup(i - 1)
                if n == 3:
                    store(i - 2)
                    if i == 0:
                        quant_x(1)
            load_dup(i)
            if i == 0:
                sort_x(2)
                load_x(3)
                load_tgt(2)
